import numpy as np
import ml_dtypes


def mxq(x, axis, fmt="e4m3"):
    dtype, down = {"e4m3": (ml_dtypes.float8_e4m3fn, 7), "e5m2": (ml_dtypes.float8_e5m2, 14)}[fmt]
    v = np.moveaxis(np.asarray(x, np.float32).astype(ml_dtypes.bfloat16).astype(np.float64), axis, -1)
    blocks = v.reshape(v.shape[:-1] + (-1, 32))
    amax = np.abs(blocks).max(-1, keepdims=True)
    byte = np.maximum(np.where(amax > 0, np.frexp(amax)[1] - 1 + 127, 0) - down, 1)
    scale = np.exp2(byte - 127.0)
    codes = (blocks / scale).astype(np.float32).astype(dtype).astype(np.float64)
    return np.moveaxis((codes * scale).reshape(v.shape), -1, axis)


WIDE = False


def mx_kscale(k):
    if not WIDE:
        return np.ones(k)
    levels = np.array([10, -10, 5, -5, 0])
    a = np.random.permutation(np.resize(levels, k // 512 * 4)).reshape(k // 512, 4)
    idx = np.arange(k)
    return np.exp2(a[idx // 512, idx % 128 // 32])


BF16 = ml_dtypes.bfloat16


def bf(x):
    return np.asarray(x, np.float32).astype(BF16)


def f64(x):
    return np.asarray(x).astype(np.float64)


E2M1 = np.array([0.0, 0.5, 1.0, 1.5, 2.0, 3.0, 4.0, 6.0, -0.0, -0.5, -1.0, -1.5, -2.0, -3.0, -4.0, -6.0])


def pack_weight(w, fmt):
    k, n = w.shape
    w = f64(bf(w)).reshape(k // 32, 32, n)
    amax = np.abs(w).max(1)
    if fmt == "e4m3":
        byte = np.frexp(amax)[1] - 1 + 127 - 7
    else:
        mant, ex = np.frexp(amax / 6.0)
        byte = np.where(mant > 0.5, ex, ex - 1) + 127
    byte = np.clip(np.where(amax > 0, byte, 1), 1, 254)
    scaled = (w * np.exp2(127.0 - byte)[:, None, :]).reshape(k, n).astype(np.float32)
    by_word = np.ascontiguousarray(scaled.reshape(k // 512, 128, 4, n).transpose(0, 1, 3, 2))
    if fmt == "e4m3":
        words = by_word.astype(ml_dtypes.float8_e4m3fn).view(np.uint8)
    else:
        c = by_word.astype(ml_dtypes.float4_e2m1fn).view(np.uint8) & 0xF
        words = c[..., 0::2] | (c[..., 1::2] << 4)
    return np.ascontiguousarray(words), np.ascontiguousarray(byte.astype(np.uint8).reshape(k // 512, 16, n))


def unpack_weight(words, scales, fmt):
    g, p, n, _ = words.shape
    if fmt == "e4m3":
        vals = np.ascontiguousarray(words).view(ml_dtypes.float8_e4m3fn).astype(np.float64)
    else:
        nib = np.empty((g, p, n, 4), np.uint8)
        nib[..., 0::2] = words & 0xF
        nib[..., 1::2] = words >> 4
        vals = E2M1[nib]
    vals = vals * np.repeat(np.exp2(scales.astype(np.float64) - 127.0), 8, axis=1)[..., None]
    return vals.transpose(0, 1, 3, 2).reshape(g * 512, n)


B, I, H = 128, 16384, 256
FMT = "e4m3"


def sigmoid(v):
    return 1.0 / (1.0 + np.exp(-v))


def setup_inputs():
    s = mx_kscale(I)
    x = bf(np.random.standard_normal((B, I)) * s)
    h_prev = bf(np.random.standard_normal((B, H)))
    c_prev = bf(np.random.standard_normal((B, H)))
    w_ih = np.random.standard_normal((4 * H, I)) * 1.0 / np.sqrt(I) / s[None, :]
    w_ih_words, w_ih_scales = pack_weight(np.ascontiguousarray(w_ih.T), FMT)
    w_hh = bf(np.random.standard_normal((4 * H, H)) * 1.0 / np.sqrt(H))
    bias_ih = bf(np.random.standard_normal(4 * H) * 0.5)
    bias_hh = bf(np.random.standard_normal(4 * H) * 0.5)
    return {"x": x,
            "h_prev": h_prev,
            "c_prev": c_prev,
            "w_ih_words": w_ih_words,
            "w_ih_scales": w_ih_scales,
            "w_hh": w_hh,
            "bias_ih": bias_ih,
            "bias_hh": bias_hh}


def reference(x, h_prev, c_prev, w_ih_words, w_ih_scales, w_hh, bias_ih, bias_hh):
    gates = (mxq(f64(x), 1, "e4m3") @ unpack_weight(w_ih_words, w_ih_scales, FMT)) + f64(bias_ih) + f64(h_prev) @ f64(w_hh).T + f64(bias_hh)
    i_g, f_g, g_g, o_g = np.split(gates, 4, axis=1)
    i_g = sigmoid(i_g)
    f_g = sigmoid(f_g)
    g_g = np.tanh(g_g)
    o_g = sigmoid(o_g)
    c_new = f_g * f64(c_prev) + i_g * g_g
    h_new = o_g * np.tanh(c_new)
    return (h_new, c_new)

@@ -1,0 +1,192 @@
+from contextlib import ExitStack
+
+import concourse.mybir as mybir
+from concourse.masks import make_identity
+
+F32 = mybir.dt.float32
+BF16 = mybir.dt.bfloat16
+I32 = mybir.dt.int32
+U32 = mybir.dt.uint32
+U8 = mybir.dt.uint8
+FP8X4 = mybir.dt.float8_e4m3fn_x4
+ACT = mybir.ActivationFunctionType
+
+P = 128
+BATCH = 128
+IN = 16384
+HID = 256
+GATES = 4 * HID
+PACK = 4
+K_PASS = P * PACK
+GROUPS = IN // K_PASS
+N_PASS = 512
+HALVES = GATES // N_PASS
+
+X_LOAD_GROUPS = 8
+BANK_GROUPS = 2
+QUANT_GROUPS = 4
+PLANES = 4
+SLOTS = GROUPS // PLANES
+W_HH_ROWS = GATES // P
+K_HALVES = HID // P
+
+FLOPS = 2 * BATCH * IN * GATES + 2 * BATCH * HID * GATES
+
+
+def tile_int8lstmcell_k_kernel(
+    tc, x, h_prev, c_prev, w_ih_words, w_ih_scales, w_hh, bias_ih, bias_hh, out_0, out_1
+):
+    nc = tc.nc
+    with ExitStack() as ctx:
+        const = ctx.enter_context(tc.tile_pool(name="const", bufs=1))
+        x_pool = ctx.enter_context(tc.tile_pool(name="x_pool", bufs=GROUPS // X_LOAD_GROUPS))
+        w_pool = ctx.enter_context(tc.tile_pool(name="w_pool", bufs=GROUPS))
+        stage = ctx.enter_context(tc.tile_pool(name="stage", bufs=2))
+        tail = ctx.enter_context(tc.tile_pool(name="tail", bufs=1))
+        psum_t = ctx.enter_context(tc.psum_pool(name="psum_t", bufs=4))
+        psum_rec = ctx.enter_context(tc.psum_pool(name="psum_rec", bufs=HALVES))
+        psum_acc = ctx.enter_context(tc.psum_pool(name="psum_acc", bufs=1))
+
+        w_scales = const.tile([P, SLOTS, GATES], U8, align_bytes=64)
+        nc.vector.memset(w_scales[:].bitcast(I32), 0)
+
+        bias_rows = const.tile([P, GATES], BF16)
+        nc.vector.memset(bias_rows[:], 0.0)
+        ones = const.tile([P, BATCH], BF16)
+        nc.vector.memset(ones[:], 1.0)
+
+        ident_f32 = const.tile([P, P], F32)
+        make_identity(nc, ident_f32[:])
+        ident_bf16 = const.tile([P, P], BF16)
+        make_identity(nc, ident_bf16[:])
+
+        h_sb = const.tile([P, HID], BF16)
+        nc.scalar.dma_start(out=h_sb[:], in_=h_prev)
+        w_hh_sb = const.tile([P, W_HH_ROWS, HID], BF16)
+        nc.scalar.dma_start(out=w_hh_sb[:], in_=w_hh.rearrange("(p r) k -> p r k", r=W_HH_ROWS))
+        c_sb = const.tile([P, HID], BF16)
+        nc.scalar.dma_start(out=c_sb[:], in_=c_prev)
+        nc.scalar.dma_start(out=bias_rows[0:1, :], in_=bias_ih.unsqueeze(0))
+        nc.scalar.dma_start(out=bias_rows[1:2, :], in_=bias_hh.unsqueeze(0))
+
+        warm = const.tile([P, 1], F32)
+        nc.vector.memset(warm[:], 0.0)
+        nc.scalar.activation(out=warm[:], in_=warm[:], func=ACT.Sigmoid)
+
+        x_tiles = []
+        for c in range(GROUPS // X_LOAD_GROUPS):
+            x_sb = x_pool.tile([P, X_LOAD_GROUPS * K_PASS], BF16)
+            nc.sync.dma_start(
+                out=x_sb[:], in_=x[:, c * X_LOAD_GROUPS * K_PASS : (c + 1) * X_LOAD_GROUPS * K_PASS]
+            )
+            x_tiles.append(x_sb)
+
+        for slot in range(SLOTS):
+            for quadrant in range(4):
+                nc.sync.dma_start(
+                    out=w_scales[32 * quadrant : 32 * quadrant + 4 * PLANES, slot, :].bitcast(I32),
+                    in_=w_ih_scales[
+                        PLANES * slot : PLANES * (slot + 1), 4 * quadrant : 4 * quadrant + 4, :
+                    ].bitcast(I32),
+                )
+
+        w_tiles = []
+        for g in range(GROUPS):
+            w_codes = w_pool.tile([P, PACK * GATES], U8, align_bytes=64)
+            nc.sync.dma_start(
+                out=w_codes[:].bitcast(I32),
+                in_=w_ih_words[g].rearrange("p n t -> p (n t)").bitcast(I32),
+            )
+            w_tiles.append(w_codes)
+
+        w_hh_t = const.tile([P, K_HALVES, GATES], BF16)
+        for kh in range(K_HALVES):
+            w_hh_ps = psum_t.tile([P, W_HH_ROWS, P], BF16, tag="transposed")
+            for r in range(W_HH_ROWS):
+                nc.tensor.transpose(w_hh_ps[:, r, :], w_hh_sb[:, r, kh * P : (kh + 1) * P], ident_bf16[:])
+            nc.vector.tensor_copy(
+                out=w_hh_t[:, kh, :].rearrange("k (p r) -> k p r", r=W_HH_ROWS),
+                in_=w_hh_ps[:].rearrange("k r p -> k p r"),
+            )
+        h_ps = psum_t.tile([P, K_HALVES, BATCH], BF16, tag="transposed")
+        for kh in range(K_HALVES):
+            nc.tensor.transpose(h_ps[:, kh, :], h_sb[:, kh * P : (kh + 1) * P], ident_bf16[:])
+        h_t = const.tile([P, K_HALVES, BATCH], BF16)
+        nc.vector.tensor_copy(out=h_t[:], in_=h_ps[:])
+
+        x_codes = const.tile([P, GROUPS, BATCH], U32, align_bytes=64)
+        x_scales = const.tile([P, GROUPS, BATCH], U8, align_bytes=64)
+        for first in range(0, GROUPS, QUANT_GROUPS):
+            grouped = stage.tile([P, QUANT_GROUPS * BATCH * PACK], BF16, align_bytes=64)
+            grouped_words = grouped[:].bitcast(F32).rearrange("p (g b u) -> p g b u", g=QUANT_GROUPS, u=2)
+            for bank in range(0, QUANT_GROUPS, BANK_GROUPS):
+                x_ps = psum_t.tile([P, BANK_GROUPS, 2, BATCH], F32, tag="transposed")
+                for j in range(BANK_GROUPS):
+                    load, g_in_load = divmod(first + bank + j, X_LOAD_GROUPS)
+                    x_words = x_tiles[load][:].bitcast(F32)
+                    for u in range(2):
+                        nc.tensor.transpose(
+                            x_ps[:, j, u, :],
+                            x_words[:, 256 * g_in_load + u : 256 * (g_in_load + 1) : 2],
+                            ident_f32[:],
+                        )
+                nc.scalar.copy(
+                    out=grouped_words[:, bank : bank + BANK_GROUPS],
+                    in_=x_ps[:].rearrange("p g u b -> p g b u"),
+                )
+            nc.vector.quantize_mx(
+                out=x_codes[:, first : first + QUANT_GROUPS, :].rearrange("p g b -> p (g b)").bitcast(FP8X4),
+                scales=x_scales[:, first : first + QUANT_GROUPS, :].rearrange("p g b -> p (g b)"),
+                in_=grouped[:],
+            )
+
+        recurrent = tail.tile([P, GATES], F32)
+        for half in range(HALVES):
+            cols = slice(half * N_PASS, (half + 1) * N_PASS)
+            rec_ps = psum_rec.tile([P, N_PASS], F32)
+            for kh in range(K_HALVES):
+                nc.tensor.matmul(
+                    rec_ps[:], lhsT=h_t[:, kh, :], rhs=w_hh_t[:, kh, cols], start=(kh == 0), stop=False
+                )
+            nc.tensor.matmul(rec_ps[:], lhsT=ones[:], rhs=bias_rows[:, cols], start=False, stop=True)
+            nc.vector.tensor_copy(out=recurrent[:, cols], in_=rec_ps[:])
+
+        acc_if = psum_acc.tile([P, N_PASS], F32)
+        acc_go = psum_acc.tile([P, N_PASS], F32)
+        for g in range(GROUPS):
+            slot, plane = divmod(g, PLANES)
+            for half, acc in enumerate((acc_if, acc_go)):
+                nc.tensor.matmul_mx(
+                    out=acc[:],
+                    lhsT=x_codes[:, g, :].bitcast(FP8X4),
+                    lhsT_scale=x_scales[:, g, :],
+                    rhs=w_tiles[g][:, PACK * half * N_PASS : PACK * (half + 1) * N_PASS].bitcast(FP8X4),
+                    rhs_scale=w_scales[4 * plane : P, slot, half * N_PASS : (half + 1) * N_PASS],
+                    start=(g == 0),
+                    stop=(g == GROUPS - 1),
+                )
+
+        gates = tail.tile([P, GATES], F32)
+        nc.vector.tensor_add(out=gates[:, 0:N_PASS], in0=acc_if[:], in1=recurrent[:, 0:N_PASS])
+        nc.vector.tensor_add(out=gates[:, N_PASS:GATES], in0=acc_go[:], in1=recurrent[:, N_PASS:GATES])
+
+        i_f = tail.tile([P, 2 * HID], F32)
+        nc.scalar.activation(out=i_f[:], in_=gates[:, 0 : 2 * HID], func=ACT.Sigmoid)
+        g_gate = tail.tile([P, HID], F32)
+        nc.scalar.activation(out=g_gate[:], in_=gates[:, 2 * HID : 3 * HID], func=ACT.Tanh)
+        o_gate = tail.tile([P, HID], F32)
+        nc.scalar.activation(out=o_gate[:], in_=gates[:, 3 * HID : 4 * HID], func=ACT.Sigmoid)
+
+        kept = tail.tile([P, HID], F32)
+        nc.vector.tensor_mul(out=kept[:], in0=i_f[:, HID : 2 * HID], in1=c_sb[:])
+        added = tail.tile([P, HID], F32)
+        nc.vector.tensor_mul(out=added[:], in0=i_f[:, 0:HID], in1=g_gate[:])
+        c_new = tail.tile([P, HID], F32)
+        nc.vector.tensor_add(out=c_new[:], in0=kept[:], in1=added[:])
+        nc.sync.dma_start(out=out_1, in_=c_new[:])
+
+        tanh_c = tail.tile([P, HID], F32)
+        nc.scalar.activation(out=tanh_c[:], in_=c_new[:], func=ACT.Tanh)
+        h_new = tail.tile([P, HID], F32)
+        nc.vector.tensor_mul(out=h_new[:], in0=o_gate[:], in1=tanh_c[:])
+        nc.sync.dma_start(out=out_0, in_=h_new[:])

@@ -81,15 +81,6 @@ def tile_int8lstmcell_k_kernel(
             )
             x_tiles.append(x_sb)
 
-        for slot in range(SLOTS):
-            for quadrant in range(4):
-                nc.sync.dma_start(
-                    out=w_scales[32 * quadrant : 32 * quadrant + 4 * PLANES, slot, :].bitcast(I32),
-                    in_=w_ih_scales[
-                        PLANES * slot : PLANES * (slot + 1), 4 * quadrant : 4 * quadrant + 4, :
-                    ].bitcast(I32),
-                )
-
         w_tiles = []
         for g in range(GROUPS):
             w_codes = w_pool.tile([P, PACK * GATES], U8, align_bytes=64)
@@ -98,6 +89,15 @@ def tile_int8lstmcell_k_kernel(
                 in_=w_ih_words[g].rearrange("p n t -> p (n t)").bitcast(I32),
             )
             w_tiles.append(w_codes)
+
+        for slot in range(SLOTS):
+            for quadrant in range(4):
+                nc.gpsimd.dma_start(
+                    out=w_scales[32 * quadrant : 32 * quadrant + 4 * PLANES, slot, :].bitcast(F32),
+                    in_=w_ih_scales[
+                        PLANES * slot : PLANES * (slot + 1), 4 * quadrant : 4 * quadrant + 4, :
+                    ].bitcast(F32),
+                )
 
         w_hh_t = const.tile([P, K_HALVES, GATES], BF16)
         for kh in range(K_HALVES):

@@ -19,8 +19,8 @@ GATES = 4 * HID
 PACK = 4
 K_PASS = P * PACK
 GROUPS = IN // K_PASS
-N_PASS = 512
-HALVES = GATES // N_PASS
+BANK = 512
+HALVES = GATES // BANK
 
 X_LOAD_GROUPS = 8
 BANK_GROUPS = 2
@@ -29,6 +29,9 @@ PLANES = 4
 SLOTS = GROUPS // PLANES
 W_HH_ROWS = GATES // P
 K_HALVES = HID // P
+BLOCKS = ((0, 2 * HID), (2 * HID, HID), (3 * HID, HID))
+LATE_GROUPS = PLANES
+FIRST_LATE = GROUPS - LATE_GROUPS
 
 FLOPS = 2 * BATCH * IN * GATES + 2 * BATCH * HID * GATES
 
@@ -43,9 +46,10 @@ def tile_int8lstmcell_k_kernel(
         w_pool = ctx.enter_context(tc.tile_pool(name="w_pool", bufs=GROUPS))
         stage = ctx.enter_context(tc.tile_pool(name="stage", bufs=2))
         tail = ctx.enter_context(tc.tile_pool(name="tail", bufs=1))
-        psum_t = ctx.enter_context(tc.psum_pool(name="psum_t", bufs=4))
+        psum_t = ctx.enter_context(tc.psum_pool(name="psum_t", bufs=3))
         psum_rec = ctx.enter_context(tc.psum_pool(name="psum_rec", bufs=HALVES))
         psum_acc = ctx.enter_context(tc.psum_pool(name="psum_acc", bufs=1))
+        ctx.enter_context(tc.manual_schedule())
 
         w_scales = const.tile([P, SLOTS, GATES], U8, align_bytes=64)
         nc.vector.memset(w_scales[:].bitcast(I32), 0)
@@ -81,23 +85,33 @@ def tile_int8lstmcell_k_kernel(
             )
             x_tiles.append(x_sb)
 
+        def load_scales(slot, quadrant):
+            nc.sync.dma_start(
+                out=w_scales[32 * quadrant : 32 * quadrant + 4 * PLANES, slot, :].bitcast(I32),
+                in_=w_ih_scales[
+                    PLANES * slot : PLANES * (slot + 1), 4 * quadrant : 4 * quadrant + 4, :
+                ].bitcast(I32),
+            )
+
+        def load_codes(g, first_col, width):
+            part = slice(PACK * first_col, PACK * (first_col + width))
+            nc.sync.dma_start(
+                out=w_tiles[g][:, part].bitcast(I32),
+                in_=w_ih_words[g].rearrange("p n t -> p (n t)")[:, part].bitcast(I32),
+            )
+
         w_tiles = []
         for g in range(GROUPS):
             w_codes = w_pool.tile([P, PACK * GATES], U8, align_bytes=64)
-            nc.sync.dma_start(
-                out=w_codes[:].bitcast(I32),
-                in_=w_ih_words[g].rearrange("p n t -> p (n t)").bitcast(I32),
-            )
             w_tiles.append(w_codes)
-
-        for slot in range(SLOTS):
-            for quadrant in range(4):
-                nc.gpsimd.dma_start(
-                    out=w_scales[32 * quadrant : 32 * quadrant + 4 * PLANES, slot, :].bitcast(F32),
-                    in_=w_ih_scales[
-                        PLANES * slot : PLANES * (slot + 1), 4 * quadrant : 4 * quadrant + 4, :
-                    ].bitcast(F32),
-                )
+        for quadrant in range(4):
+            load_scales(0, quadrant)
+        for g in range(FIRST_LATE):
+            load_codes(g, 0, GATES)
+            load_scales(g // PLANES + 1, g % PLANES)
+        for first_col, width in BLOCKS:
+            for g in range(FIRST_LATE, GROUPS):
+                load_codes(g, first_col, width)
 
         w_hh_t = const.tile([P, K_HALVES, GATES], BF16)
         for kh in range(K_HALVES):
@@ -142,8 +156,8 @@ def tile_int8lstmcell_k_kernel(
 
         recurrent = tail.tile([P, GATES], F32)
         for half in range(HALVES):
-            cols = slice(half * N_PASS, (half + 1) * N_PASS)
-            rec_ps = psum_rec.tile([P, N_PASS], F32)
+            cols = slice(half * BANK, (half + 1) * BANK)
+            rec_ps = psum_rec.tile([P, BANK], F32)
             for kh in range(K_HALVES):
                 nc.tensor.matmul(
                     rec_ps[:], lhsT=h_t[:, kh, :], rhs=w_hh_t[:, kh, cols], start=(kh == 0), stop=False
@@ -151,31 +165,40 @@ def tile_int8lstmcell_k_kernel(
             nc.tensor.matmul(rec_ps[:], lhsT=ones[:], rhs=bias_rows[:, cols], start=False, stop=True)
             nc.vector.tensor_copy(out=recurrent[:, cols], in_=rec_ps[:])
 
-        acc_if = psum_acc.tile([P, N_PASS], F32)
-        acc_go = psum_acc.tile([P, N_PASS], F32)
-        for g in range(GROUPS):
+        acc_if = psum_acc.tile([P, 2 * HID], F32)
+        acc_g = psum_acc.tile([P, HID], F32)
+        acc_o = psum_acc.tile([P, HID], F32)
+        accs = (acc_if, acc_g, acc_o)
+
+        def mx_pass(g, block):
+            acc = accs[block]
+            first_col, width = BLOCKS[block]
             slot, plane = divmod(g, PLANES)
-            for half, acc in enumerate((acc_if, acc_go)):
-                nc.tensor.matmul_mx(
-                    out=acc[:],
-                    lhsT=x_codes[:, g, :].bitcast(FP8X4),
-                    lhsT_scale=x_scales[:, g, :],
-                    rhs=w_tiles[g][:, PACK * half * N_PASS : PACK * (half + 1) * N_PASS].bitcast(FP8X4),
-                    rhs_scale=w_scales[4 * plane : P, slot, half * N_PASS : (half + 1) * N_PASS],
-                    start=(g == 0),
-                    stop=(g == GROUPS - 1),
-                )
+            nc.tensor.matmul_mx(
+                out=acc[:],
+                lhsT=x_codes[:, g, :].bitcast(FP8X4),
+                lhsT_scale=x_scales[:, g, :],
+                rhs=w_tiles[g][:, PACK * first_col : PACK * (first_col + width)].bitcast(FP8X4),
+                rhs_scale=w_scales[4 * plane : P, slot, first_col : first_col + width],
+                start=(g == 0),
+                stop=(g == GROUPS - 1),
+            )
+
+        for g in range(FIRST_LATE):
+            for block in range(len(BLOCKS)):
+                mx_pass(g, block)
+        for block in range(len(BLOCKS)):
+            for g in range(FIRST_LATE, GROUPS):
+                mx_pass(g, block)
 
         gates = tail.tile([P, GATES], F32)
-        nc.vector.tensor_add(out=gates[:, 0:N_PASS], in0=acc_if[:], in1=recurrent[:, 0:N_PASS])
-        nc.vector.tensor_add(out=gates[:, N_PASS:GATES], in0=acc_go[:], in1=recurrent[:, N_PASS:GATES])
+        nc.vector.tensor_add(out=gates[:, 0 : 2 * HID], in0=acc_if[:], in1=recurrent[:, 0 : 2 * HID])
+        nc.vector.tensor_add(out=gates[:, 2 * HID : 3 * HID], in0=acc_g[:], in1=recurrent[:, 2 * HID : 3 * HID])
 
         i_f = tail.tile([P, 2 * HID], F32)
         nc.scalar.activation(out=i_f[:], in_=gates[:, 0 : 2 * HID], func=ACT.Sigmoid)
         g_gate = tail.tile([P, HID], F32)
         nc.scalar.activation(out=g_gate[:], in_=gates[:, 2 * HID : 3 * HID], func=ACT.Tanh)
-        o_gate = tail.tile([P, HID], F32)
-        nc.scalar.activation(out=o_gate[:], in_=gates[:, 3 * HID : 4 * HID], func=ACT.Sigmoid)
 
         kept = tail.tile([P, HID], F32)
         nc.vector.tensor_mul(out=kept[:], in0=i_f[:, HID : 2 * HID], in1=c_sb[:])
@@ -187,6 +210,10 @@ def tile_int8lstmcell_k_kernel(
 
         tanh_c = tail.tile([P, HID], F32)
         nc.scalar.activation(out=tanh_c[:], in_=c_new[:], func=ACT.Tanh)
+
+        nc.vector.tensor_add(out=gates[:, 3 * HID : 4 * HID], in0=acc_o[:], in1=recurrent[:, 3 * HID : 4 * HID])
+        o_gate = tail.tile([P, HID], F32)
+        nc.scalar.activation(out=o_gate[:], in_=gates[:, 3 * HID : 4 * HID], func=ACT.Sigmoid)
         h_new = tail.tile([P, HID], F32)
         nc.vector.tensor_mul(out=h_new[:], in0=o_gate[:], in1=tanh_c[:])
         nc.sync.dma_start(out=out_0, in_=h_new[:])

@@ -104,11 +104,11 @@ def tile_int8lstmcell_k_kernel(
         for g in range(GROUPS):
             w_codes = w_pool.tile([P, PACK * GATES], U8, align_bytes=64)
             w_tiles.append(w_codes)
-        for quadrant in range(4):
-            load_scales(0, quadrant)
+        for slot in range(SLOTS):
+            for quadrant in range(4):
+                load_scales(slot, quadrant)
         for g in range(FIRST_LATE):
             load_codes(g, 0, GATES)
-            load_scales(g // PLANES + 1, g % PLANES)
         for first_col, width in BLOCKS:
             for g in range(FIRST_LATE, GROUPS):
                 load_codes(g, first_col, width)

@@ -85,12 +85,10 @@ def tile_int8lstmcell_k_kernel(
             )
             x_tiles.append(x_sb)
 
-        def load_scales(slot, quadrant):
-            nc.sync.dma_start(
-                out=w_scales[32 * quadrant : 32 * quadrant + 4 * PLANES, slot, :].bitcast(I32),
-                in_=w_ih_scales[
-                    PLANES * slot : PLANES * (slot + 1), 4 * quadrant : 4 * quadrant + 4, :
-                ].bitcast(I32),
+        def load_scales(quadrant, r):
+            nc.gpsimd.dma_start(
+                out=w_scales[32 * quadrant + r : 32 * quadrant + 4 * PLANES : 4, :, :].bitcast(F32),
+                in_=w_ih_scales.rearrange("(j s) q n -> j s q n", s=SLOTS)[:, :, 4 * quadrant + r, :].bitcast(F32),
             )
 
         def load_codes(g, first_col, width):
@@ -100,17 +98,20 @@ def tile_int8lstmcell_k_kernel(
                 in_=w_ih_words[g].rearrange("p n t -> p (n t)")[:, part].bitcast(I32),
             )
 
+        order = [SLOTS * plane + slot for slot in range(SLOTS) for plane in range(PLANES)]
+        early_groups = order[:FIRST_LATE]
+        late_groups = order[FIRST_LATE:]
         w_tiles = []
         for g in range(GROUPS):
             w_codes = w_pool.tile([P, PACK * GATES], U8, align_bytes=64)
             w_tiles.append(w_codes)
-        for slot in range(SLOTS):
-            for quadrant in range(4):
-                load_scales(slot, quadrant)
-        for g in range(FIRST_LATE):
+        for quadrant in range(4):
+            for r in range(4):
+                load_scales(quadrant, r)
+        for g in early_groups:
             load_codes(g, 0, GATES)
         for first_col, width in BLOCKS:
-            for g in range(FIRST_LATE, GROUPS):
+            for g in late_groups:
                 load_codes(g, first_col, width)
 
         w_hh_t = const.tile([P, K_HALVES, GATES], BF16)
@@ -173,22 +174,22 @@ def tile_int8lstmcell_k_kernel(
         def mx_pass(g, block):
             acc = accs[block]
             first_col, width = BLOCKS[block]
-            slot, plane = divmod(g, PLANES)
+            plane, slot = divmod(g, SLOTS)
             nc.tensor.matmul_mx(
                 out=acc[:],
                 lhsT=x_codes[:, g, :].bitcast(FP8X4),
                 lhsT_scale=x_scales[:, g, :],
                 rhs=w_tiles[g][:, PACK * first_col : PACK * (first_col + width)].bitcast(FP8X4),
                 rhs_scale=w_scales[4 * plane : P, slot, first_col : first_col + width],
-                start=(g == 0),
-                stop=(g == GROUPS - 1),
+                start=(g == order[0]),
+                stop=(g == order[-1]),
             )
 
-        for g in range(FIRST_LATE):
+        for g in early_groups:
             for block in range(len(BLOCKS)):
                 mx_pass(g, block)
         for block in range(len(BLOCKS)):
-            for g in range(FIRST_LATE, GROUPS):
+            for g in late_groups:
                 mx_pass(g, block)
 
         gates = tail.tile([P, GATES], F32)

@@ -86,9 +86,9 @@ def tile_int8lstmcell_k_kernel(
             x_tiles.append(x_sb)
 
         def load_scales(quadrant, r):
-            nc.gpsimd.dma_start(
-                out=w_scales[32 * quadrant + r : 32 * quadrant + 4 * PLANES : 4, :, :].bitcast(F32),
-                in_=w_ih_scales.rearrange("(j s) q n -> j s q n", s=SLOTS)[:, :, 4 * quadrant + r, :].bitcast(F32),
+            nc.sync.dma_start(
+                out=w_scales[32 * quadrant + r : 32 * quadrant + 4 * PLANES : 4, :, :].bitcast(I32),
+                in_=w_ih_scales.rearrange("(j s) q n -> j s q n", s=SLOTS)[:, :, 4 * quadrant + r, :].bitcast(I32),
             )
 
         def load_codes(g, first_col, width):

@@ -86,9 +86,10 @@ def tile_int8lstmcell_k_kernel(
             x_tiles.append(x_sb)
 
         def load_scales(quadrant, r):
-            nc.sync.dma_start(
-                out=w_scales[32 * quadrant + r : 32 * quadrant + 4 * PLANES : 4, :, :].bitcast(I32),
-                in_=w_ih_scales.rearrange("(j s) q n -> j s q n", s=SLOTS)[:, :, 4 * quadrant + r, :].bitcast(I32),
+            queue, word = (nc.sync, I32) if quadrant < 2 else (nc.gpsimd, F32)
+            queue.dma_start(
+                out=w_scales[32 * quadrant + r : 32 * quadrant + 4 * PLANES : 4, :, :].bitcast(word),
+                in_=w_ih_scales.rearrange("(j s) q n -> j s q n", s=SLOTS)[:, :, 4 * quadrant + r, :].bitcast(word),
             )
 
         def load_codes(g, first_col, width):

@@ -86,7 +86,7 @@ def tile_int8lstmcell_k_kernel(
             x_tiles.append(x_sb)
 
         def load_scales(quadrant, r):
-            queue, word = (nc.sync, I32) if quadrant < 2 else (nc.gpsimd, F32)
+            queue, word = (nc.sync, I32) if quadrant < 1 else (nc.gpsimd, F32)
             queue.dma_start(
                 out=w_scales[32 * quadrant + r : 32 * quadrant + 4 * PLANES : 4, :, :].bitcast(word),
                 in_=w_ih_scales.rearrange("(j s) q n -> j s q n", s=SLOTS)[:, :, 4 * quadrant + r, :].bitcast(word),
@@ -194,28 +194,38 @@ def tile_int8lstmcell_k_kernel(
                 mx_pass(g, block)
 
         gates = tail.tile([P, GATES], F32)
-        nc.vector.tensor_add(out=gates[:, 0 : 2 * HID], in0=acc_if[:], in1=recurrent[:, 0 : 2 * HID])
-        nc.vector.tensor_add(out=gates[:, 2 * HID : 3 * HID], in0=acc_g[:], in1=recurrent[:, 2 * HID : 3 * HID])
-
         i_f = tail.tile([P, 2 * HID], F32)
-        nc.scalar.activation(out=i_f[:], in_=gates[:, 0 : 2 * HID], func=ACT.Sigmoid)
         g_gate = tail.tile([P, HID], F32)
-        nc.scalar.activation(out=g_gate[:], in_=gates[:, 2 * HID : 3 * HID], func=ACT.Tanh)
-
         kept = tail.tile([P, HID], F32)
-        nc.vector.tensor_mul(out=kept[:], in0=i_f[:, HID : 2 * HID], in1=c_sb[:])
         added = tail.tile([P, HID], F32)
-        nc.vector.tensor_mul(out=added[:], in0=i_f[:, 0:HID], in1=g_gate[:])
         c_new = tail.tile([P, HID], F32)
-        nc.vector.tensor_add(out=c_new[:], in0=kept[:], in1=added[:])
-        nc.sync.dma_start(out=out_1, in_=c_new[:])
-
         tanh_c = tail.tile([P, HID], F32)
-        nc.scalar.activation(out=tanh_c[:], in_=c_new[:], func=ACT.Tanh)
-
-        nc.vector.tensor_add(out=gates[:, 3 * HID : 4 * HID], in0=acc_o[:], in1=recurrent[:, 3 * HID : 4 * HID])
         o_gate = tail.tile([P, HID], F32)
-        nc.scalar.activation(out=o_gate[:], in_=gates[:, 3 * HID : 4 * HID], func=ACT.Sigmoid)
         h_new = tail.tile([P, HID], F32)
-        nc.vector.tensor_mul(out=h_new[:], in0=o_gate[:], in1=tanh_c[:])
-        nc.sync.dma_start(out=out_0, in_=h_new[:])
+        half_cols = [slice(half * (HID // 2), (half + 1) * (HID // 2)) for half in range(2)]
+
+        def add_recurrent(acc, gate, cols):
+            into = slice(gate * HID + cols.start, gate * HID + cols.stop)
+            nc.vector.tensor_add(out=gates[:, into], in0=acc, in1=recurrent[:, into])
+            return gates[:, into]
+
+        for gate in range(2):
+            cols = slice(gate * HID, (gate + 1) * HID)
+            pre = add_recurrent(acc_if[:, cols], gate, slice(0, HID))
+            nc.scalar.activation(out=i_f[:, cols], in_=pre, func=ACT.Sigmoid)
+        for cols in half_cols:
+            pre = add_recurrent(acc_g[:, cols], 2, cols)
+            nc.scalar.activation(out=g_gate[:, cols], in_=pre, func=ACT.Tanh)
+        nc.vector.tensor_mul(out=kept[:], in0=i_f[:, HID : 2 * HID], in1=c_sb[:])
+        for cols in half_cols:
+            nc.vector.tensor_mul(out=added[:, cols], in0=i_f[:, cols], in1=g_gate[:, cols])
+        for cols in half_cols:
+            nc.vector.tensor_add(out=c_new[:, cols], in0=kept[:, cols], in1=added[:, cols])
+            nc.scalar.activation(out=tanh_c[:, cols], in_=c_new[:, cols], func=ACT.Tanh)
+        nc.sync.dma_start(out=out_1, in_=c_new[:])
+        for cols in half_cols:
+            pre = add_recurrent(acc_o[:, cols], 3, cols)
+            nc.scalar.activation(out=o_gate[:, cols], in_=pre, func=ACT.Sigmoid)
+        for cols in half_cols:
+            nc.vector.tensor_mul(out=h_new[:, cols], in0=o_gate[:, cols], in1=tanh_c[:, cols])
+            nc.sync.dma_start(out=out_0[:, cols], in_=h_new[:, cols])

@@ -22,16 +22,16 @@ GROUPS = IN // K_PASS
 BANK = 512
 HALVES = GATES // BANK
 
-X_LOAD_GROUPS = 8
+X_LOAD_GROUPS = 16
 BANK_GROUPS = 2
 QUANT_GROUPS = 4
 PLANES = 4
 SLOTS = GROUPS // PLANES
 W_HH_ROWS = GATES // P
 K_HALVES = HID // P
-BLOCKS = ((0, 2 * HID), (2 * HID, HID), (3 * HID, HID))
-LATE_GROUPS = PLANES
-FIRST_LATE = GROUPS - LATE_GROUPS
+BLOCKS = ((HID, 2 * HID), (0, HID), (3 * HID, HID))
+LOADS_BEFORE_SCALES = 3
+FIRST_LATE = (29, 29, 27)
 
 FLOPS = 2 * BATCH * IN * GATES + 2 * BATCH * HID * GATES
 
@@ -43,7 +43,7 @@ def tile_int8lstmcell_k_kernel(
     with ExitStack() as ctx:
         const = ctx.enter_context(tc.tile_pool(name="const", bufs=1))
         x_pool = ctx.enter_context(tc.tile_pool(name="x_pool", bufs=GROUPS // X_LOAD_GROUPS))
-        w_pool = ctx.enter_context(tc.tile_pool(name="w_pool", bufs=GROUPS))
+        w_pool = ctx.enter_context(tc.tile_pool(name="w_pool", bufs=1))
         stage = ctx.enter_context(tc.tile_pool(name="stage", bufs=2))
         tail = ctx.enter_context(tc.tile_pool(name="tail", bufs=1))
         psum_t = ctx.enter_context(tc.psum_pool(name="psum_t", bufs=3))
@@ -86,34 +86,47 @@ def tile_int8lstmcell_k_kernel(
             x_tiles.append(x_sb)
 
         def load_scales(quadrant, r):
-            queue, word = (nc.sync, I32) if quadrant < 1 else (nc.gpsimd, F32)
+            queue, word = (nc.sync, I32) if quadrant < 2 else (nc.gpsimd, F32)
             queue.dma_start(
                 out=w_scales[32 * quadrant + r : 32 * quadrant + 4 * PLANES : 4, :, :].bitcast(word),
-                in_=w_ih_scales.rearrange("(j s) q n -> j s q n", s=SLOTS)[:, :, 4 * quadrant + r, :].bitcast(word),
+                in_=w_ih_scales.rearrange("(s j) q n -> j s q n", j=PLANES)[:, :, 4 * quadrant + r, :].bitcast(word),
             )
 
-        def load_codes(g, first_col, width):
-            part = slice(PACK * first_col, PACK * (first_col + width))
+        w_blocks = {}
+
+        def load_codes(first_group, groups, blocks):
+            first_col = min(BLOCKS[block][0] for block in blocks)
+            cols = sum(BLOCKS[block][1] for block in blocks)
+            w_codes = w_pool.tile(
+                [P, groups, PACK * cols], U8, align_bytes=64, name=f"w_codes_{first_group}_{first_col}"
+            )
             nc.sync.dma_start(
-                out=w_tiles[g][:, part].bitcast(I32),
-                in_=w_ih_words[g].rearrange("p n t -> p (n t)")[:, part].bitcast(I32),
+                out=w_codes[:].bitcast(I32),
+                in_=w_ih_words[first_group : first_group + groups]
+                .rearrange("g p n t -> p g (n t)")[:, :, PACK * first_col : PACK * (first_col + cols)]
+                .bitcast(I32),
             )
+            for j in range(groups):
+                for block in blocks:
+                    start = PACK * (BLOCKS[block][0] - first_col)
+                    w_blocks[first_group + j, block] = w_codes[:, j, start : start + PACK * BLOCKS[block][1]]
 
-        order = [SLOTS * plane + slot for slot in range(SLOTS) for plane in range(PLANES)]
-        early_groups = order[:FIRST_LATE]
-        late_groups = order[FIRST_LATE:]
-        w_tiles = []
-        for g in range(GROUPS):
-            w_codes = w_pool.tile([P, PACK * GATES], U8, align_bytes=64)
-            w_tiles.append(w_codes)
-        for quadrant in range(4):
+        for quadrant in (0, 2, 3):
             for r in range(4):
                 load_scales(quadrant, r)
-        for g in early_groups:
-            load_codes(g, 0, GATES)
-        for first_col, width in BLOCKS:
-            for g in late_groups:
-                load_codes(g, first_col, width)
+        steps = []
+        for g in range(GROUPS):
+            early = [block for block in range(len(BLOCKS)) if g < FIRST_LATE[block]]
+            if early:
+                steps.append((g, early))
+        for block, first in enumerate(FIRST_LATE):
+            steps += [(g, [block]) for g in range(first, GROUPS)]
+        for g, blocks in steps[:LOADS_BEFORE_SCALES]:
+            load_codes(g, 1, blocks)
+        for r in range(4):
+            load_scales(1, r)
+        for g, blocks in steps[LOADS_BEFORE_SCALES:]:
+            load_codes(g, 1, blocks)
 
         w_hh_t = const.tile([P, K_HALVES, GATES], BF16)
         for kh in range(K_HALVES):
@@ -167,34 +180,32 @@ def tile_int8lstmcell_k_kernel(
             nc.tensor.matmul(rec_ps[:], lhsT=ones[:], rhs=bias_rows[:, cols], start=False, stop=True)
             nc.vector.tensor_copy(out=recurrent[:, cols], in_=rec_ps[:])
 
-        acc_if = psum_acc.tile([P, 2 * HID], F32)
-        acc_g = psum_acc.tile([P, HID], F32)
+        acc_fg = psum_acc.tile([P, 2 * HID], F32)
+        acc_i = psum_acc.tile([P, HID], F32)
         acc_o = psum_acc.tile([P, HID], F32)
-        accs = (acc_if, acc_g, acc_o)
+        accs = (acc_fg, acc_i, acc_o)
 
         def mx_pass(g, block):
             acc = accs[block]
             first_col, width = BLOCKS[block]
-            plane, slot = divmod(g, SLOTS)
+            slot, plane = divmod(g, PLANES)
             nc.tensor.matmul_mx(
                 out=acc[:],
                 lhsT=x_codes[:, g, :].bitcast(FP8X4),
                 lhsT_scale=x_scales[:, g, :],
-                rhs=w_tiles[g][:, PACK * first_col : PACK * (first_col + width)].bitcast(FP8X4),
+                rhs=w_blocks[g, block].bitcast(FP8X4),
                 rhs_scale=w_scales[4 * plane : P, slot, first_col : first_col + width],
-                start=(g == order[0]),
-                stop=(g == order[-1]),
+                start=(g == 0),
+                stop=(g == GROUPS - 1),
             )
 
-        for g in early_groups:
-            for block in range(len(BLOCKS)):
-                mx_pass(g, block)
-        for block in range(len(BLOCKS)):
-            for g in late_groups:
+        for g, blocks in steps:
+            for block in blocks:
                 mx_pass(g, block)
 
         gates = tail.tile([P, GATES], F32)
-        i_f = tail.tile([P, 2 * HID], F32)
+        i_gate = tail.tile([P, HID], F32)
+        f_gate = tail.tile([P, HID], F32)
         g_gate = tail.tile([P, HID], F32)
         kept = tail.tile([P, HID], F32)
         added = tail.tile([P, HID], F32)
@@ -209,16 +220,16 @@ def tile_int8lstmcell_k_kernel(
             nc.vector.tensor_add(out=gates[:, into], in0=acc, in1=recurrent[:, into])
             return gates[:, into]
 
-        for gate in range(2):
-            cols = slice(gate * HID, (gate + 1) * HID)
-            pre = add_recurrent(acc_if[:, cols], gate, slice(0, HID))
-            nc.scalar.activation(out=i_f[:, cols], in_=pre, func=ACT.Sigmoid)
+        pre = add_recurrent(acc_fg[:, 0:HID], 1, slice(0, HID))
+        nc.scalar.activation(out=f_gate[:], in_=pre, func=ACT.Sigmoid)
+        pre = add_recurrent(acc_fg[:, HID : 2 * HID], 2, slice(0, HID))
+        nc.scalar.activation(out=g_gate[:], in_=pre, func=ACT.Tanh)
         for cols in half_cols:
-            pre = add_recurrent(acc_g[:, cols], 2, cols)
-            nc.scalar.activation(out=g_gate[:, cols], in_=pre, func=ACT.Tanh)
-        nc.vector.tensor_mul(out=kept[:], in0=i_f[:, HID : 2 * HID], in1=c_sb[:])
+            pre = add_recurrent(acc_i[:, cols], 0, cols)
+            nc.scalar.activation(out=i_gate[:, cols], in_=pre, func=ACT.Sigmoid)
+        nc.vector.tensor_mul(out=kept[:], in0=f_gate[:], in1=c_sb[:])
         for cols in half_cols:
-            nc.vector.tensor_mul(out=added[:, cols], in0=i_f[:, cols], in1=g_gate[:, cols])
+            nc.vector.tensor_mul(out=added[:, cols], in0=i_gate[:, cols], in1=g_gate[:, cols])
         for cols in half_cols:
             nc.vector.tensor_add(out=c_new[:, cols], in0=kept[:, cols], in1=added[:, cols])
             nc.scalar.activation(out=tanh_c[:, cols], in_=c_new[:, cols], func=ACT.Tanh)

from contextlib import ExitStack

import concourse.mybir as mybir
from concourse.masks import make_identity

F32 = mybir.dt.float32
BF16 = mybir.dt.bfloat16
I32 = mybir.dt.int32
U32 = mybir.dt.uint32
U8 = mybir.dt.uint8
FP8X4 = mybir.dt.float8_e4m3fn_x4
ACT = mybir.ActivationFunctionType

P = 128
BATCH = 128
IN = 16384
HID = 256
GATES = 4 * HID
PACK = 4
K_PASS = P * PACK
GROUPS = IN // K_PASS
BANK = 512
HALVES = GATES // BANK

X_LOAD_GROUPS = 16
BANK_GROUPS = 2
QUANT_GROUPS = 4
PLANES = 4
SLOTS = GROUPS // PLANES
W_HH_ROWS = GATES // P
K_HALVES = HID // P
BLOCKS = ((HID, 2 * HID), (0, HID), (3 * HID, HID))
LOADS_BEFORE_SCALES = 3
FIRST_LATE = (29, 29, 27)

FLOPS = 2 * BATCH * IN * GATES + 2 * BATCH * HID * GATES


def tile_int8lstmcell_k_kernel(
    tc, x, h_prev, c_prev, w_ih_words, w_ih_scales, w_hh, bias_ih, bias_hh, out_0, out_1
):
    nc = tc.nc
    with ExitStack() as ctx:
        const = ctx.enter_context(tc.tile_pool(name="const", bufs=1))
        x_pool = ctx.enter_context(tc.tile_pool(name="x_pool", bufs=GROUPS // X_LOAD_GROUPS))
        w_pool = ctx.enter_context(tc.tile_pool(name="w_pool", bufs=1))
        stage = ctx.enter_context(tc.tile_pool(name="stage", bufs=2))
        tail = ctx.enter_context(tc.tile_pool(name="tail", bufs=1))
        psum_t = ctx.enter_context(tc.psum_pool(name="psum_t", bufs=3))
        psum_rec = ctx.enter_context(tc.psum_pool(name="psum_rec", bufs=HALVES))
        psum_acc = ctx.enter_context(tc.psum_pool(name="psum_acc", bufs=1))
        ctx.enter_context(tc.manual_schedule())

        w_scales = const.tile([P, SLOTS, GATES], U8, align_bytes=64)
        nc.vector.memset(w_scales[:].bitcast(I32), 0)

        bias_rows = const.tile([P, GATES], BF16)
        nc.vector.memset(bias_rows[:], 0.0)
        ones = const.tile([P, BATCH], BF16)
        nc.vector.memset(ones[:], 1.0)

        ident_f32 = const.tile([P, P], F32)
        make_identity(nc, ident_f32[:])
        ident_bf16 = const.tile([P, P], BF16)
        make_identity(nc, ident_bf16[:])

        h_sb = const.tile([P, HID], BF16)
        nc.scalar.dma_start(out=h_sb[:], in_=h_prev)
        w_hh_sb = const.tile([P, W_HH_ROWS, HID], BF16)
        nc.scalar.dma_start(out=w_hh_sb[:], in_=w_hh.rearrange("(p r) k -> p r k", r=W_HH_ROWS))
        c_sb = const.tile([P, HID], BF16)
        nc.scalar.dma_start(out=c_sb[:], in_=c_prev)
        nc.scalar.dma_start(out=bias_rows[0:1, :], in_=bias_ih.unsqueeze(0))
        nc.scalar.dma_start(out=bias_rows[1:2, :], in_=bias_hh.unsqueeze(0))

        warm = const.tile([P, 1], F32)
        nc.vector.memset(warm[:], 0.0)
        nc.scalar.activation(out=warm[:], in_=warm[:], func=ACT.Sigmoid)

        x_tiles = []
        for c in range(GROUPS // X_LOAD_GROUPS):
            x_sb = x_pool.tile([P, X_LOAD_GROUPS * K_PASS], BF16)
            nc.sync.dma_start(
                out=x_sb[:], in_=x[:, c * X_LOAD_GROUPS * K_PASS : (c + 1) * X_LOAD_GROUPS * K_PASS]
            )
            x_tiles.append(x_sb)

        def load_scales(quadrant, r):
            queue, word = (nc.sync, I32) if quadrant < 2 else (nc.gpsimd, F32)
            queue.dma_start(
                out=w_scales[32 * quadrant + r : 32 * quadrant + 4 * PLANES : 4, :, :].bitcast(word),
                in_=w_ih_scales.rearrange("(s j) q n -> j s q n", j=PLANES)[:, :, 4 * quadrant + r, :].bitcast(word),
            )

        w_blocks = {}

        def load_codes(first_group, groups, blocks):
            first_col = min(BLOCKS[block][0] for block in blocks)
            cols = sum(BLOCKS[block][1] for block in blocks)
            w_codes = w_pool.tile(
                [P, groups, PACK * cols], U8, align_bytes=64, name=f"w_codes_{first_group}_{first_col}"
            )
            nc.sync.dma_start(
                out=w_codes[:].bitcast(I32),
                in_=w_ih_words[first_group : first_group + groups]
                .rearrange("g p n t -> p g (n t)")[:, :, PACK * first_col : PACK * (first_col + cols)]
                .bitcast(I32),
            )
            for j in range(groups):
                for block in blocks:
                    start = PACK * (BLOCKS[block][0] - first_col)
                    w_blocks[first_group + j, block] = w_codes[:, j, start : start + PACK * BLOCKS[block][1]]

        for quadrant in (0, 2, 3):
            for r in range(4):
                load_scales(quadrant, r)
        steps = []
        for g in range(GROUPS):
            early = [block for block in range(len(BLOCKS)) if g < FIRST_LATE[block]]
            if early:
                steps.append((g, early))
        for block, first in enumerate(FIRST_LATE):
            steps += [(g, [block]) for g in range(first, GROUPS)]
        for g, blocks in steps[:LOADS_BEFORE_SCALES]:
            load_codes(g, 1, blocks)
        for r in range(4):
            load_scales(1, r)
        for g, blocks in steps[LOADS_BEFORE_SCALES:]:
            load_codes(g, 1, blocks)

        w_hh_t = const.tile([P, K_HALVES, GATES], BF16)
        for kh in range(K_HALVES):
            w_hh_ps = psum_t.tile([P, W_HH_ROWS, P], BF16, tag="transposed")
            for r in range(W_HH_ROWS):
                nc.tensor.transpose(w_hh_ps[:, r, :], w_hh_sb[:, r, kh * P : (kh + 1) * P], ident_bf16[:])
            nc.vector.tensor_copy(
                out=w_hh_t[:, kh, :].rearrange("k (p r) -> k p r", r=W_HH_ROWS),
                in_=w_hh_ps[:].rearrange("k r p -> k p r"),
            )
        h_ps = psum_t.tile([P, K_HALVES, BATCH], BF16, tag="transposed")
        for kh in range(K_HALVES):
            nc.tensor.transpose(h_ps[:, kh, :], h_sb[:, kh * P : (kh + 1) * P], ident_bf16[:])
        h_t = const.tile([P, K_HALVES, BATCH], BF16)
        nc.vector.tensor_copy(out=h_t[:], in_=h_ps[:])

        x_codes = const.tile([P, GROUPS, BATCH], U32, align_bytes=64)
        x_scales = const.tile([P, GROUPS, BATCH], U8, align_bytes=64)
        for first in range(0, GROUPS, QUANT_GROUPS):
            grouped = stage.tile([P, QUANT_GROUPS * BATCH * PACK], BF16, align_bytes=64)
            grouped_words = grouped[:].bitcast(F32).rearrange("p (g b u) -> p g b u", g=QUANT_GROUPS, u=2)
            for bank in range(0, QUANT_GROUPS, BANK_GROUPS):
                x_ps = psum_t.tile([P, BANK_GROUPS, 2, BATCH], F32, tag="transposed")
                for j in range(BANK_GROUPS):
                    load, g_in_load = divmod(first + bank + j, X_LOAD_GROUPS)
                    x_words = x_tiles[load][:].bitcast(F32)
                    for u in range(2):
                        nc.tensor.transpose(
                            x_ps[:, j, u, :],
                            x_words[:, 256 * g_in_load + u : 256 * (g_in_load + 1) : 2],
                            ident_f32[:],
                        )
                nc.scalar.copy(
                    out=grouped_words[:, bank : bank + BANK_GROUPS],
                    in_=x_ps[:].rearrange("p g u b -> p g b u"),
                )
            nc.vector.quantize_mx(
                out=x_codes[:, first : first + QUANT_GROUPS, :].rearrange("p g b -> p (g b)").bitcast(FP8X4),
                scales=x_scales[:, first : first + QUANT_GROUPS, :].rearrange("p g b -> p (g b)"),
                in_=grouped[:],
            )

        recurrent = tail.tile([P, GATES], F32)
        for half in range(HALVES):
            cols = slice(half * BANK, (half + 1) * BANK)
            rec_ps = psum_rec.tile([P, BANK], F32)
            for kh in range(K_HALVES):
                nc.tensor.matmul(
                    rec_ps[:], lhsT=h_t[:, kh, :], rhs=w_hh_t[:, kh, cols], start=(kh == 0), stop=False
                )
            nc.tensor.matmul(rec_ps[:], lhsT=ones[:], rhs=bias_rows[:, cols], start=False, stop=True)
            nc.vector.tensor_copy(out=recurrent[:, cols], in_=rec_ps[:])

        acc_fg = psum_acc.tile([P, 2 * HID], F32)
        acc_i = psum_acc.tile([P, HID], F32)
        acc_o = psum_acc.tile([P, HID], F32)
        accs = (acc_fg, acc_i, acc_o)

        def mx_pass(g, block):
            acc = accs[block]
            first_col, width = BLOCKS[block]
            slot, plane = divmod(g, PLANES)
            nc.tensor.matmul_mx(
                out=acc[:],
                lhsT=x_codes[:, g, :].bitcast(FP8X4),
                lhsT_scale=x_scales[:, g, :],
                rhs=w_blocks[g, block].bitcast(FP8X4),
                rhs_scale=w_scales[4 * plane : P, slot, first_col : first_col + width],
                start=(g == 0),
                stop=(g == GROUPS - 1),
            )

        for g, blocks in steps:
            for block in blocks:
                mx_pass(g, block)

        gates = tail.tile([P, GATES], F32)
        i_gate = tail.tile([P, HID], F32)
        f_gate = tail.tile([P, HID], F32)
        g_gate = tail.tile([P, HID], F32)
        kept = tail.tile([P, HID], F32)
        added = tail.tile([P, HID], F32)
        c_new = tail.tile([P, HID], F32)
        tanh_c = tail.tile([P, HID], F32)
        o_gate = tail.tile([P, HID], F32)
        h_new = tail.tile([P, HID], F32)
        half_cols = [slice(half * (HID // 2), (half + 1) * (HID // 2)) for half in range(2)]

        def add_recurrent(acc, gate, cols):
            into = slice(gate * HID + cols.start, gate * HID + cols.stop)
            nc.vector.tensor_add(out=gates[:, into], in0=acc, in1=recurrent[:, into])
            return gates[:, into]

        pre = add_recurrent(acc_fg[:, 0:HID], 1, slice(0, HID))
        nc.scalar.activation(out=f_gate[:], in_=pre, func=ACT.Sigmoid)
        pre = add_recurrent(acc_fg[:, HID : 2 * HID], 2, slice(0, HID))
        nc.scalar.activation(out=g_gate[:], in_=pre, func=ACT.Tanh)
        for cols in half_cols:
            pre = add_recurrent(acc_i[:, cols], 0, cols)
            nc.scalar.activation(out=i_gate[:, cols], in_=pre, func=ACT.Sigmoid)
        nc.vector.tensor_mul(out=kept[:], in0=f_gate[:], in1=c_sb[:])
        for cols in half_cols:
            nc.vector.tensor_mul(out=added[:, cols], in0=i_gate[:, cols], in1=g_gate[:, cols])
        for cols in half_cols:
            nc.vector.tensor_add(out=c_new[:, cols], in0=kept[:, cols], in1=added[:, cols])
            nc.scalar.activation(out=tanh_c[:, cols], in_=c_new[:, cols], func=ACT.Tanh)
        nc.sync.dma_start(out=out_1, in_=c_new[:])
        for cols in half_cols:
            pre = add_recurrent(acc_o[:, cols], 3, cols)
            nc.scalar.activation(out=o_gate[:, cols], in_=pre, func=ACT.Sigmoid)
        for cols in half_cols:
            nc.vector.tensor_mul(out=h_new[:, cols], in0=o_gate[:, cols], in1=tanh_c[:, cols])
            nc.sync.dma_start(out=out_0[:, cols], in_=h_new[:, cols])
